import numpy as np
import ml_dtypes


def mxq(x, axis, fmt="e4m3"):
    dtype, down = {"e4m3": (ml_dtypes.float8_e4m3fn, 7), "e5m2": (ml_dtypes.float8_e5m2, 14)}[fmt]
    v = np.moveaxis(np.asarray(x, np.float32).astype(ml_dtypes.bfloat16).astype(np.float64), axis, -1)
    blocks = v.reshape(v.shape[:-1] + (-1, 32))
    amax = np.abs(blocks).max(-1, keepdims=True)
    byte = np.maximum(np.where(amax > 0, np.frexp(amax)[1] - 1 + 127, 0) - down, 1)
    scale = np.exp2(byte - 127.0)
    codes = (blocks / scale).astype(np.float32).astype(dtype).astype(np.float64)
    return np.moveaxis((codes * scale).reshape(v.shape), -1, axis)


WIDE = False


def mx_kscale(k):
    if not WIDE:
        return np.ones(k)
    levels = np.array([10, -10, 5, -5, 0])
    if k % 512:
        return np.exp2(np.random.permutation(np.resize(levels, k // 32))).repeat(32)
    a = np.empty((k // 512, 16))
    for p in range(k // 512):
        a[p, :8] = np.random.permutation(np.resize(levels, 8))
        for g in range(8):
            far = levels[np.abs(levels - a[p, g]) >= 10]
            a[p, g + 8] = far[np.random.randint(len(far))]
    return np.exp2(a.ravel()).repeat(32)


BF16 = ml_dtypes.bfloat16


def bf(x):
    return np.asarray(x, np.float32).astype(BF16)


def f64(x):
    return np.asarray(x).astype(np.float64)


B, D_IN, D_OUT = 128, 1024, 1024
EPS = 0.01


def setup_inputs():
    s, t = mx_kscale(D_IN), mx_kscale(D_OUT)
    return {"x": bf(np.random.standard_normal((B, D_IN)) * s),
            "W": bf(np.random.standard_normal((D_OUT, D_IN)) / np.sqrt(D_IN) / s[None, :] * t[:, None]),
            "b": bf(np.random.standard_normal(D_OUT) * 0.3 * t),
            "g": bf(np.random.standard_normal((D_OUT, D_OUT)) / np.sqrt(D_OUT) / t[None, :]),
            "g_bias": bf(np.random.standard_normal(D_OUT) * 0.3)}


def reference(x, W, b, g, g_bias):
    h = (mxq(f64(x), 1, "e4m3") @ mxq(f64(W), 1, "e4m3").T) + f64(b)
    c = np.cos((mxq(h, 1, "e4m3") @ mxq(f64(g), 1, "e4m3").T) + f64(g_bias))
    return np.where(np.abs(c) < EPS, -c, c)

@@ -1,0 +1,250 @@
+import math
+from contextlib import ExitStack
+
+import concourse.mybir as mybir
+from concourse.masks import make_identity
+
+F32 = mybir.dt.float32
+BF16 = mybir.dt.bfloat16
+U32 = mybir.dt.uint32
+U8 = mybir.dt.uint8
+FP8X4 = mybir.dt.float8_e4m3fn_x4
+ALU = mybir.AluOpType
+ACT = mybir.ActivationFunctionType
+
+P = 128
+PACK = 4
+K_PASS = P * PACK
+BATCH = 128
+D = 1024
+PASSES = D // K_PASS
+CHUNKS = D // P
+ROW_WORDS = D // 2
+CHUNK_CODES = PASSES * P
+PAIR = 2 * P
+BANK = 512
+
+EPS = 0.01
+TURN = 2.0 * math.pi
+ROUND = 1.5 * 2.0**23
+
+FLOPS = 2 * 2 * BATCH * D * D
+
+
+def tile_onehiddenlayer_s_kernel(tc, x, W, b, g, g_bias, out):
+    nc = tc.nc
+    with ExitStack() as ctx:
+        keep = ctx.enter_context(tc.tile_pool(name="keep", bufs=1))
+        work = ctx.enter_context(tc.tile_pool(name="work", bufs=D // PAIR))
+        psum_turned = ctx.enter_context(tc.psum_pool(name="psum_turned", bufs=4))
+        psum_h = ctx.enter_context(tc.psum_pool(name="psum_h", bufs=PASSES))
+        psum_z = ctx.enter_context(tc.psum_pool(name="psum_z", bufs=2))
+
+        x_rows = keep.tile([P, D], BF16)
+        w_rows = keep.tile([P, CHUNKS * D], BF16)
+        g_rows = keep.tile([P, CHUNKS * D], BF16)
+        x_grouped = keep.tile([P, D], BF16, align_bytes=64)
+        w_grouped = keep.tile([P, CHUNKS * D], BF16, align_bytes=64)
+        g_grouped = keep.tile([P, CHUNKS * D], BF16, align_bytes=64)
+        h_grouped = keep.tile([P, D], BF16, align_bytes=64)
+        x_codes = keep.tile([P, CHUNK_CODES], U32, align_bytes=64)
+        x_scales = keep.tile([P, CHUNK_CODES], U8, align_bytes=64)
+        w_codes = keep.tile([P, CHUNKS * CHUNK_CODES], U32, align_bytes=64)
+        w_scales = keep.tile([P, CHUNKS * CHUNK_CODES], U8, align_bytes=64)
+        g_codes = keep.tile([P, CHUNKS * CHUNK_CODES], U32, align_bytes=64)
+        g_scales = keep.tile([P, CHUNKS * CHUNK_CODES], U8, align_bytes=64)
+        h_codes = keep.tile([P, CHUNK_CODES], U32, align_bytes=64)
+        h_scales = keep.tile([P, CHUNK_CODES], U8, align_bytes=64)
+
+        ident = keep.tile([P, P], F32)
+        ones = keep.tile([P, P], BF16)
+        b_as_rows = keep.tile([P, K_PASS], BF16)
+        g_bias_as_row = keep.tile([P, D], BF16)
+        b_by_partition = keep.tile([P, CHUNKS], F32)
+        g_bias_turns = keep.tile([P, D], F32)
+        zero_column = keep.tile([P, 1], F32)
+        sine_of_zero = keep.tile([P, 1], F32)
+
+        ctx.enter_context(tc.manual_schedule())
+
+        nc.vector.memset(b_as_rows[:], 0.0)
+        nc.vector.memset(g_bias_as_row[:], 0.0)
+        nc.vector.memset(zero_column[:], 0.0)
+        nc.vector.memset(ones[:], 1.0)
+        make_identity(nc, ident[:])
+        nc.scalar.activation(out=sine_of_zero[:], in_=zero_column[:], func=ACT.Sin)
+
+        nc.sync.dma_start(out=x_rows[:], in_=x)
+        nc.sync.dma_start(out=b_as_rows[0:PASSES, :], in_=b.rearrange("(s q) -> s q", q=K_PASS))
+        nc.sync.dma_start(out=g_bias_as_row[0:1, :], in_=g_bias.rearrange("(o n) -> o n", o=1))
+        w_pairs = W.rearrange("(s p u e) k -> s u p (e k)", s=PASSES, p=P, u=2, e=2)
+        for a in range(CHUNKS // 2):
+            nc.sync.dma_start(out=w_rows[:, a * 2 * D : (a + 1) * 2 * D], in_=w_pairs[a // 2, a % 2])
+        for i in range(CHUNKS):
+            nc.sync.dma_start(out=g_rows[:, i * D : (i + 1) * D], in_=g[i * P : (i + 1) * P, :])
+
+        def turn_chunk(rows, grouped, i, on_vector):
+            row_words = rows[:].bitcast(F32)[:, i * ROW_WORDS : (i + 1) * ROW_WORDS]
+            grouped_words = grouped[:].bitcast(F32)[:, i * ROW_WORDS : (i + 1) * ROW_WORDS]
+            turned = psum_turned.tile([P, PASSES, 2, P], F32)
+            for s in range(PASSES):
+                for u in range(2):
+                    words = slice(2 * s * P + u, 2 * (s + 1) * P, 2)
+                    nc.tensor.transpose(turned[:, s, u, :], row_words[:, words], ident[:])
+            side_by_side = turned[:].rearrange("p s u r -> p s r u")
+            contiguous = grouped_words.rearrange("p (s r u) -> p s r u", s=PASSES, r=P, u=2)
+            if on_vector:
+                nc.vector.tensor_copy(out=contiguous, in_=side_by_side)
+            else:
+                nc.scalar.copy(out=contiguous, in_=side_by_side)
+
+        def quantise_chunk(grouped, codes, scales, i):
+            nc.vector.quantize_mx(
+                out=codes[:, i * CHUNK_CODES : (i + 1) * CHUNK_CODES].bitcast(FP8X4),
+                scales=scales[:, i * CHUNK_CODES : (i + 1) * CHUNK_CODES],
+                in_=grouped[:, i * D : (i + 1) * D],
+            )
+
+        def multiply(acc, left_codes, left_scales, left_chunk, right_codes, right_scales, right_chunk):
+            for s in range(PASSES):
+                left = slice(left_chunk * CHUNK_CODES + s * P, left_chunk * CHUNK_CODES + (s + 1) * P)
+                right = slice(right_chunk * CHUNK_CODES + s * P, right_chunk * CHUNK_CODES + (s + 1) * P)
+                nc.tensor.matmul_mx(
+                    out=acc,
+                    lhsT=left_codes[:, left].bitcast(FP8X4),
+                    lhsT_scale=left_scales[:, left],
+                    rhs=right_codes[:, right].bitcast(FP8X4),
+                    rhs_scale=right_scales[:, right],
+                    start=(s == 0),
+                    stop=(s == PASSES - 1),
+                )
+
+        turn_chunk(x_rows, x_grouped, 0, on_vector=True)
+        b_turned = psum_turned.tile([P, 2, P], F32, tag="turned")
+        for u in range(2):
+            nc.tensor.transpose(b_turned[:, u, :], b_as_rows[:].bitcast(F32)[:, u : 2 * P : 2], ident[:])
+        nc.vector.tensor_copy(
+            out=b_by_partition[:].rearrange("p (s u e) -> p s u e", s=PASSES, u=2),
+            in_=b_turned[:, :, 0:PASSES].bitcast(BF16).rearrange("p u (s e) -> p s u e", e=2),
+        )
+        quantise_chunk(x_grouped, x_codes, x_scales, 0)
+        for half in range(D // BANK):
+            cols = slice(half * BANK, (half + 1) * BANK)
+            spread = psum_z.tile([P, BANK], F32, tag="z")
+            nc.tensor.matmul(out=spread[:], lhsT=ones[:], rhs=g_bias_as_row[:, cols], start=True, stop=True)
+            nc.vector.tensor_scalar(
+                out=g_bias_turns[:, cols], in0=spread[:],
+                scalar1=1.0 / TURN, scalar2=0.25, op0=ALU.mult, op1=ALU.add,
+            )
+
+        def is_w(n):
+            return 0 <= n < CHUNKS
+
+        def is_g(n):
+            return CHUNKS <= n < 2 * CHUNKS
+
+        def turn(n):
+            if is_w(n):
+                turn_chunk(w_rows, w_grouped, n, on_vector=False)
+            if is_g(n):
+                turn_chunk(g_rows, g_grouped, n - CHUNKS, on_vector=False)
+
+        def quantise(n):
+            if is_w(n):
+                quantise_chunk(w_grouped, w_codes, w_scales, n)
+            if is_g(n):
+                quantise_chunk(g_grouped, g_codes, g_scales, n - CHUNKS)
+
+        h_turned = {}
+
+        def first_product(n):
+            if not (is_w(n) and n % 2 == 1):
+                return
+            s2 = n // PACK
+            if n % PACK == 1:
+                bank = psum_h.tile([P, PACK, BATCH], F32)
+                h_turned[s2] = bank
+            for i in (n - 1, n):
+                multiply(h_turned[s2][:, i % PACK, :], w_codes, w_scales, i, x_codes, x_scales, 0)
+            if n % PACK == PACK - 1:
+                nc.vector.tensor_tensor(
+                    out=h_grouped[:, s2 * K_PASS : (s2 + 1) * K_PASS].rearrange("p (r t) -> p r t", t=PACK),
+                    in0=h_turned[s2][:].rearrange("p t r -> p r t"),
+                    in1=b_by_partition[:, s2 * PACK : (s2 + 1) * PACK]
+                    .unsqueeze(1)
+                    .to_broadcast([P, BATCH, PACK]),
+                    op=ALU.add,
+                )
+                nc.vector.quantize_mx(
+                    out=h_codes[:, s2 * BATCH : (s2 + 1) * BATCH].bitcast(FP8X4),
+                    scales=h_scales[:, s2 * BATCH : (s2 + 1) * BATCH],
+                    in_=h_grouped[:, s2 * K_PASS : (s2 + 1) * K_PASS],
+                )
+
+        turns = {}
+        shifted = {}
+        cosine = {}
+        cosine_size = {}
+        sign_plus_one = {}
+
+        def second_product(n):
+            if not (is_g(n) and n % 2 == 1):
+                return
+            z = psum_z.tile([P, PAIR], F32, tag="z")
+            for e in range(2):
+                multiply(z[:, e * P : (e + 1) * P], h_codes, h_scales, 0, g_codes, g_scales, n - CHUNKS - 1 + e)
+            first_column = (n - CHUNKS - 1) * P
+            angle = work.tile([P, PAIR], F32)
+            nc.vector.scalar_tensor_tensor(
+                out=angle[:], in0=z[:], scalar=1.0 / TURN,
+                in1=g_bias_turns[:, first_column : first_column + PAIR],
+                op0=ALU.mult, op1=ALU.add,
+            )
+            whole = work.tile([P, PAIR], F32)
+            nc.scalar.activation(out=whole[:], in_=angle[:], func=ACT.Copy, bias=ROUND, scale=1.0)
+            turns[n] = angle
+            shifted[n] = whole
+
+        def sine(n):
+            if n not in turns:
+                return
+            minus_fraction = work.tile([P, PAIR], F32)
+            nc.vector.scalar_tensor_tensor(
+                out=minus_fraction[:], in0=shifted[n][:], scalar=ROUND, in1=turns[n][:],
+                op0=ALU.subtract, op1=ALU.subtract,
+            )
+            c = work.tile([P, PAIR], F32)
+            nc.scalar.activation(out=c[:], in_=minus_fraction[:], func=ACT.Sin, scale=-TURN)
+            c_size = work.tile([P, PAIR], F32)
+            nc.scalar.activation(out=c_size[:], in_=c[:], func=ACT.Abs)
+            cosine[n] = c
+            cosine_size[n] = c_size
+
+        def compare(n):
+            if n not in cosine:
+                return
+            stays = work.tile([P, PAIR], F32)
+            nc.vector.tensor_scalar(
+                out=stays[:], in0=cosine_size[n][:], scalar1=EPS, scalar2=2.0, op0=ALU.is_ge, op1=ALU.mult
+            )
+            sign_plus_one[n] = stays
+
+        def flip(n):
+            if n not in sign_plus_one:
+                return
+            first_column = (n - CHUNKS - 1) * P
+            flipped = work.tile([P, PAIR], F32)
+            nc.vector.scalar_tensor_tensor(
+                out=flipped[:], in0=sign_plus_one[n][:], scalar=1.0, in1=cosine[n][:],
+                op0=ALU.subtract, op1=ALU.mult,
+            )
+            nc.sync.dma_start(out=out[:, first_column : first_column + PAIR], in_=flipped[:])
+
+        for step in range(2 * CHUNKS + 11):
+            turn(step)
+            quantise(step - 2)
+            first_product(step - 4)
+            second_product(step - 5)
+            sine(step - 7)
+            compare(step - 9)
+            flip(step - 11)

@@ -35,7 +35,7 @@ def tile_onehiddenlayer_s_kernel(tc, x, W, b, g, g_bias, out):
     nc = tc.nc
     with ExitStack() as ctx:
         keep = ctx.enter_context(tc.tile_pool(name="keep", bufs=1))
-        work = ctx.enter_context(tc.tile_pool(name="work", bufs=D // PAIR))
+        work = ctx.enter_context(tc.tile_pool(name="work", bufs=D // PAIR + 1))
         psum_turned = ctx.enter_context(tc.psum_pool(name="psum_turned", bufs=4))
         psum_h = ctx.enter_context(tc.psum_pool(name="psum_h", bufs=PASSES))
         psum_z = ctx.enter_context(tc.psum_pool(name="psum_z", bufs=2))
@@ -175,6 +175,10 @@ def tile_onehiddenlayer_s_kernel(tc, x, W, b, g, g_bias, out):
                     .to_broadcast([P, BATCH, PACK]),
                     op=ALU.add,
                 )
+
+        def quantise_h(n):
+            if is_w(n) and n % PACK == PACK - 1:
+                s2 = n // PACK
                 nc.vector.quantize_mx(
                     out=h_codes[:, s2 * BATCH : (s2 + 1) * BATCH].bitcast(FP8X4),
                     scales=h_scales[:, s2 * BATCH : (s2 + 1) * BATCH],
@@ -187,64 +191,81 @@ def tile_onehiddenlayer_s_kernel(tc, x, W, b, g, g_bias, out):
         cosine_size = {}
         sign_plus_one = {}
 
+        def columns(n):
+            if not is_g(n) or (n % 2 == 0 and n < 2 * CHUNKS - 2):
+                return None
+            last = (n - CHUNKS + 1) * P
+            return slice(last - P if n >= 2 * CHUNKS - 2 else last - PAIR, last)
+
         def second_product(n):
-            if not (is_g(n) and n % 2 == 1):
+            cols = columns(n)
+            if cols is None:
                 return
+            width = cols.stop - cols.start
             z = psum_z.tile([P, PAIR], F32, tag="z")
-            for e in range(2):
-                multiply(z[:, e * P : (e + 1) * P], h_codes, h_scales, 0, g_codes, g_scales, n - CHUNKS - 1 + e)
-            first_column = (n - CHUNKS - 1) * P
+            for e in range(width // P):
+                multiply(z[:, e * P : (e + 1) * P], h_codes, h_scales, 0, g_codes, g_scales, cols.start // P + e)
             angle = work.tile([P, PAIR], F32)
             nc.vector.scalar_tensor_tensor(
-                out=angle[:], in0=z[:], scalar=1.0 / TURN,
-                in1=g_bias_turns[:, first_column : first_column + PAIR],
+                out=angle[:, 0:width], in0=z[:, 0:width], scalar=1.0 / TURN, in1=g_bias_turns[:, cols],
                 op0=ALU.mult, op1=ALU.add,
             )
             whole = work.tile([P, PAIR], F32)
-            nc.scalar.activation(out=whole[:], in_=angle[:], func=ACT.Copy, bias=ROUND, scale=1.0)
-            turns[n] = angle
-            shifted[n] = whole
+            nc.scalar.activation(
+                out=whole[:, 0:width], in_=angle[:, 0:width], func=ACT.Copy, bias=ROUND, scale=1.0
+            )
+            turns[n] = angle[:, 0:width]
+            shifted[n] = whole[:, 0:width]
 
         def sine(n):
             if n not in turns:
                 return
+            width = turns[n].shape[1]
             minus_fraction = work.tile([P, PAIR], F32)
             nc.vector.scalar_tensor_tensor(
-                out=minus_fraction[:], in0=shifted[n][:], scalar=ROUND, in1=turns[n][:],
+                out=minus_fraction[:, 0:width], in0=shifted[n], scalar=ROUND, in1=turns[n],
                 op0=ALU.subtract, op1=ALU.subtract,
             )
             c = work.tile([P, PAIR], F32)
-            nc.scalar.activation(out=c[:], in_=minus_fraction[:], func=ACT.Sin, scale=-TURN)
-            c_size = work.tile([P, PAIR], F32)
-            nc.scalar.activation(out=c_size[:], in_=c[:], func=ACT.Abs)
-            cosine[n] = c
-            cosine_size[n] = c_size
+            nc.scalar.activation(out=c[:, 0:width], in_=minus_fraction[:, 0:width], func=ACT.Sin, scale=-TURN)
+            cosine[n] = c[:, 0:width]
 
-        def compare(n):
+        def size(n):
             if n not in cosine:
                 return
+            c_size = work.tile([P, PAIR], F32)
+            width = cosine[n].shape[1]
+            nc.scalar.activation(out=c_size[:, 0:width], in_=cosine[n], func=ACT.Abs)
+            cosine_size[n] = c_size[:, 0:width]
+
+        def compare(n):
+            if n not in cosine_size:
+                return
             stays = work.tile([P, PAIR], F32)
+            width = cosine_size[n].shape[1]
             nc.vector.tensor_scalar(
-                out=stays[:], in0=cosine_size[n][:], scalar1=EPS, scalar2=2.0, op0=ALU.is_ge, op1=ALU.mult
+                out=stays[:, 0:width], in0=cosine_size[n], scalar1=EPS, scalar2=2.0, op0=ALU.is_ge, op1=ALU.mult
             )
-            sign_plus_one[n] = stays
+            sign_plus_one[n] = stays[:, 0:width]
 
         def flip(n):
             if n not in sign_plus_one:
                 return
-            first_column = (n - CHUNKS - 1) * P
             flipped = work.tile([P, PAIR], F32)
+            width = cosine[n].shape[1]
             nc.vector.scalar_tensor_tensor(
-                out=flipped[:], in0=sign_plus_one[n][:], scalar=1.0, in1=cosine[n][:],
+                out=flipped[:, 0:width], in0=sign_plus_one[n], scalar=1.0, in1=cosine[n],
                 op0=ALU.subtract, op1=ALU.mult,
             )
-            nc.sync.dma_start(out=out[:, first_column : first_column + PAIR], in_=flipped[:])
+            nc.sync.dma_start(out=out[:, columns(n)], in_=flipped[:, 0:width])
 
         for step in range(2 * CHUNKS + 11):
             turn(step)
             quantise(step - 2)
             first_product(step - 4)
+            quantise_h(step - 5)
             second_product(step - 5)
             sine(step - 7)
-            compare(step - 9)
+            size(step - 8)
+            compare(step - 10)
             flip(step - 11)

@@ -67,8 +67,8 @@ def tile_onehiddenlayer_s_kernel(tc, x, W, b, g, g_bias, out):
 
         ctx.enter_context(tc.manual_schedule())
 
-        nc.vector.memset(b_as_rows[:], 0.0)
-        nc.vector.memset(g_bias_as_row[:], 0.0)
+        nc.vector.memset(b_as_rows[:].bitcast(F32), 0.0)
+        nc.vector.memset(g_bias_as_row[:].bitcast(F32), 0.0)
         nc.vector.memset(zero_column[:], 0.0)
         nc.vector.memset(ones[:], 1.0)
         make_identity(nc, ident[:])

import math
from contextlib import ExitStack

import concourse.mybir as mybir
from concourse.masks import make_identity

F32 = mybir.dt.float32
BF16 = mybir.dt.bfloat16
U32 = mybir.dt.uint32
U8 = mybir.dt.uint8
FP8X4 = mybir.dt.float8_e4m3fn_x4
ALU = mybir.AluOpType
ACT = mybir.ActivationFunctionType

P = 128
PACK = 4
K_PASS = P * PACK
BATCH = 128
D = 1024
PASSES = D // K_PASS
CHUNKS = D // P
ROW_WORDS = D // 2
CHUNK_CODES = PASSES * P
PAIR = 2 * P
BANK = 512

EPS = 0.01
TURN = 2.0 * math.pi
ROUND = 1.5 * 2.0**23

FLOPS = 2 * 2 * BATCH * D * D


def tile_onehiddenlayer_s_kernel(tc, x, W, b, g, g_bias, out):
    nc = tc.nc
    with ExitStack() as ctx:
        keep = ctx.enter_context(tc.tile_pool(name="keep", bufs=1))
        work = ctx.enter_context(tc.tile_pool(name="work", bufs=D // PAIR + 1))
        psum_turned = ctx.enter_context(tc.psum_pool(name="psum_turned", bufs=4))
        psum_h = ctx.enter_context(tc.psum_pool(name="psum_h", bufs=PASSES))
        psum_z = ctx.enter_context(tc.psum_pool(name="psum_z", bufs=2))

        x_rows = keep.tile([P, D], BF16)
        w_rows = keep.tile([P, CHUNKS * D], BF16)
        g_rows = keep.tile([P, CHUNKS * D], BF16)
        x_grouped = keep.tile([P, D], BF16, align_bytes=64)
        w_grouped = keep.tile([P, CHUNKS * D], BF16, align_bytes=64)
        g_grouped = keep.tile([P, CHUNKS * D], BF16, align_bytes=64)
        h_grouped = keep.tile([P, D], BF16, align_bytes=64)
        x_codes = keep.tile([P, CHUNK_CODES], U32, align_bytes=64)
        x_scales = keep.tile([P, CHUNK_CODES], U8, align_bytes=64)
        w_codes = keep.tile([P, CHUNKS * CHUNK_CODES], U32, align_bytes=64)
        w_scales = keep.tile([P, CHUNKS * CHUNK_CODES], U8, align_bytes=64)
        g_codes = keep.tile([P, CHUNKS * CHUNK_CODES], U32, align_bytes=64)
        g_scales = keep.tile([P, CHUNKS * CHUNK_CODES], U8, align_bytes=64)
        h_codes = keep.tile([P, CHUNK_CODES], U32, align_bytes=64)
        h_scales = keep.tile([P, CHUNK_CODES], U8, align_bytes=64)

        ident = keep.tile([P, P], F32)
        ones = keep.tile([P, P], BF16)
        b_as_rows = keep.tile([P, K_PASS], BF16)
        g_bias_as_row = keep.tile([P, D], BF16)
        b_by_partition = keep.tile([P, CHUNKS], F32)
        g_bias_turns = keep.tile([P, D], F32)
        zero_column = keep.tile([P, 1], F32)
        sine_of_zero = keep.tile([P, 1], F32)

        ctx.enter_context(tc.manual_schedule())

        nc.vector.memset(b_as_rows[:].bitcast(F32), 0.0)
        nc.vector.memset(g_bias_as_row[:].bitcast(F32), 0.0)
        nc.vector.memset(zero_column[:], 0.0)
        nc.vector.memset(ones[:], 1.0)
        make_identity(nc, ident[:])
        nc.scalar.activation(out=sine_of_zero[:], in_=zero_column[:], func=ACT.Sin)

        nc.sync.dma_start(out=x_rows[:], in_=x)
        nc.sync.dma_start(out=b_as_rows[0:PASSES, :], in_=b.rearrange("(s q) -> s q", q=K_PASS))
        nc.sync.dma_start(out=g_bias_as_row[0:1, :], in_=g_bias.rearrange("(o n) -> o n", o=1))
        w_pairs = W.rearrange("(s p u e) k -> s u p (e k)", s=PASSES, p=P, u=2, e=2)
        for a in range(CHUNKS // 2):
            nc.sync.dma_start(out=w_rows[:, a * 2 * D : (a + 1) * 2 * D], in_=w_pairs[a // 2, a % 2])
        for i in range(CHUNKS):
            nc.sync.dma_start(out=g_rows[:, i * D : (i + 1) * D], in_=g[i * P : (i + 1) * P, :])

        def turn_chunk(rows, grouped, i, on_vector):
            row_words = rows[:].bitcast(F32)[:, i * ROW_WORDS : (i + 1) * ROW_WORDS]
            grouped_words = grouped[:].bitcast(F32)[:, i * ROW_WORDS : (i + 1) * ROW_WORDS]
            turned = psum_turned.tile([P, PASSES, 2, P], F32)
            for s in range(PASSES):
                for u in range(2):
                    words = slice(2 * s * P + u, 2 * (s + 1) * P, 2)
                    nc.tensor.transpose(turned[:, s, u, :], row_words[:, words], ident[:])
            side_by_side = turned[:].rearrange("p s u r -> p s r u")
            contiguous = grouped_words.rearrange("p (s r u) -> p s r u", s=PASSES, r=P, u=2)
            if on_vector:
                nc.vector.tensor_copy(out=contiguous, in_=side_by_side)
            else:
                nc.scalar.copy(out=contiguous, in_=side_by_side)

        def quantise_chunk(grouped, codes, scales, i):
            nc.vector.quantize_mx(
                out=codes[:, i * CHUNK_CODES : (i + 1) * CHUNK_CODES].bitcast(FP8X4),
                scales=scales[:, i * CHUNK_CODES : (i + 1) * CHUNK_CODES],
                in_=grouped[:, i * D : (i + 1) * D],
            )

        def multiply(acc, left_codes, left_scales, left_chunk, right_codes, right_scales, right_chunk):
            for s in range(PASSES):
                left = slice(left_chunk * CHUNK_CODES + s * P, left_chunk * CHUNK_CODES + (s + 1) * P)
                right = slice(right_chunk * CHUNK_CODES + s * P, right_chunk * CHUNK_CODES + (s + 1) * P)
                nc.tensor.matmul_mx(
                    out=acc,
                    lhsT=left_codes[:, left].bitcast(FP8X4),
                    lhsT_scale=left_scales[:, left],
                    rhs=right_codes[:, right].bitcast(FP8X4),
                    rhs_scale=right_scales[:, right],
                    start=(s == 0),
                    stop=(s == PASSES - 1),
                )

        turn_chunk(x_rows, x_grouped, 0, on_vector=True)
        b_turned = psum_turned.tile([P, 2, P], F32, tag="turned")
        for u in range(2):
            nc.tensor.transpose(b_turned[:, u, :], b_as_rows[:].bitcast(F32)[:, u : 2 * P : 2], ident[:])
        nc.vector.tensor_copy(
            out=b_by_partition[:].rearrange("p (s u e) -> p s u e", s=PASSES, u=2),
            in_=b_turned[:, :, 0:PASSES].bitcast(BF16).rearrange("p u (s e) -> p s u e", e=2),
        )
        quantise_chunk(x_grouped, x_codes, x_scales, 0)
        for half in range(D // BANK):
            cols = slice(half * BANK, (half + 1) * BANK)
            spread = psum_z.tile([P, BANK], F32, tag="z")
            nc.tensor.matmul(out=spread[:], lhsT=ones[:], rhs=g_bias_as_row[:, cols], start=True, stop=True)
            nc.vector.tensor_scalar(
                out=g_bias_turns[:, cols], in0=spread[:],
                scalar1=1.0 / TURN, scalar2=0.25, op0=ALU.mult, op1=ALU.add,
            )

        def is_w(n):
            return 0 <= n < CHUNKS

        def is_g(n):
            return CHUNKS <= n < 2 * CHUNKS

        def turn(n):
            if is_w(n):
                turn_chunk(w_rows, w_grouped, n, on_vector=False)
            if is_g(n):
                turn_chunk(g_rows, g_grouped, n - CHUNKS, on_vector=False)

        def quantise(n):
            if is_w(n):
                quantise_chunk(w_grouped, w_codes, w_scales, n)
            if is_g(n):
                quantise_chunk(g_grouped, g_codes, g_scales, n - CHUNKS)

        h_turned = {}

        def first_product(n):
            if not (is_w(n) and n % 2 == 1):
                return
            s2 = n // PACK
            if n % PACK == 1:
                bank = psum_h.tile([P, PACK, BATCH], F32)
                h_turned[s2] = bank
            for i in (n - 1, n):
                multiply(h_turned[s2][:, i % PACK, :], w_codes, w_scales, i, x_codes, x_scales, 0)
            if n % PACK == PACK - 1:
                nc.vector.tensor_tensor(
                    out=h_grouped[:, s2 * K_PASS : (s2 + 1) * K_PASS].rearrange("p (r t) -> p r t", t=PACK),
                    in0=h_turned[s2][:].rearrange("p t r -> p r t"),
                    in1=b_by_partition[:, s2 * PACK : (s2 + 1) * PACK]
                    .unsqueeze(1)
                    .to_broadcast([P, BATCH, PACK]),
                    op=ALU.add,
                )

        def quantise_h(n):
            if is_w(n) and n % PACK == PACK - 1:
                s2 = n // PACK
                nc.vector.quantize_mx(
                    out=h_codes[:, s2 * BATCH : (s2 + 1) * BATCH].bitcast(FP8X4),
                    scales=h_scales[:, s2 * BATCH : (s2 + 1) * BATCH],
                    in_=h_grouped[:, s2 * K_PASS : (s2 + 1) * K_PASS],
                )

        turns = {}
        shifted = {}
        cosine = {}
        cosine_size = {}
        sign_plus_one = {}

        def columns(n):
            if not is_g(n) or (n % 2 == 0 and n < 2 * CHUNKS - 2):
                return None
            last = (n - CHUNKS + 1) * P
            return slice(last - P if n >= 2 * CHUNKS - 2 else last - PAIR, last)

        def second_product(n):
            cols = columns(n)
            if cols is None:
                return
            width = cols.stop - cols.start
            z = psum_z.tile([P, PAIR], F32, tag="z")
            for e in range(width // P):
                multiply(z[:, e * P : (e + 1) * P], h_codes, h_scales, 0, g_codes, g_scales, cols.start // P + e)
            angle = work.tile([P, PAIR], F32)
            nc.vector.scalar_tensor_tensor(
                out=angle[:, 0:width], in0=z[:, 0:width], scalar=1.0 / TURN, in1=g_bias_turns[:, cols],
                op0=ALU.mult, op1=ALU.add,
            )
            whole = work.tile([P, PAIR], F32)
            nc.scalar.activation(
                out=whole[:, 0:width], in_=angle[:, 0:width], func=ACT.Copy, bias=ROUND, scale=1.0
            )
            turns[n] = angle[:, 0:width]
            shifted[n] = whole[:, 0:width]

        def sine(n):
            if n not in turns:
                return
            width = turns[n].shape[1]
            minus_fraction = work.tile([P, PAIR], F32)
            nc.vector.scalar_tensor_tensor(
                out=minus_fraction[:, 0:width], in0=shifted[n], scalar=ROUND, in1=turns[n],
                op0=ALU.subtract, op1=ALU.subtract,
            )
            c = work.tile([P, PAIR], F32)
            nc.scalar.activation(out=c[:, 0:width], in_=minus_fraction[:, 0:width], func=ACT.Sin, scale=-TURN)
            cosine[n] = c[:, 0:width]

        def size(n):
            if n not in cosine:
                return
            c_size = work.tile([P, PAIR], F32)
            width = cosine[n].shape[1]
            nc.scalar.activation(out=c_size[:, 0:width], in_=cosine[n], func=ACT.Abs)
            cosine_size[n] = c_size[:, 0:width]

        def compare(n):
            if n not in cosine_size:
                return
            stays = work.tile([P, PAIR], F32)
            width = cosine_size[n].shape[1]
            nc.vector.tensor_scalar(
                out=stays[:, 0:width], in0=cosine_size[n], scalar1=EPS, scalar2=2.0, op0=ALU.is_ge, op1=ALU.mult
            )
            sign_plus_one[n] = stays[:, 0:width]

        def flip(n):
            if n not in sign_plus_one:
                return
            flipped = work.tile([P, PAIR], F32)
            width = cosine[n].shape[1]
            nc.vector.scalar_tensor_tensor(
                out=flipped[:, 0:width], in0=sign_plus_one[n], scalar=1.0, in1=cosine[n],
                op0=ALU.subtract, op1=ALU.mult,
            )
            nc.sync.dma_start(out=out[:, columns(n)], in_=flipped[:, 0:width])

        for step in range(2 * CHUNKS + 11):
            turn(step)
            quantise(step - 2)
            first_product(step - 4)
            quantise_h(step - 5)
            second_product(step - 5)
            sine(step - 7)
            size(step - 8)
            compare(step - 10)
            flip(step - 11)
